import numpy as np
import ml_dtypes


def mxq(x, axis, fmt="e4m3"):
    dtype, down = {"e4m3": (ml_dtypes.float8_e4m3fn, 7), "e5m2": (ml_dtypes.float8_e5m2, 14)}[fmt]
    v = np.moveaxis(np.asarray(x, np.float32).astype(ml_dtypes.bfloat16).astype(np.float64), axis, -1)
    blocks = v.reshape(v.shape[:-1] + (-1, 32))
    amax = np.abs(blocks).max(-1, keepdims=True)
    byte = np.maximum(np.where(amax > 0, np.frexp(amax)[1] - 1 + 127, 0) - down, 1)
    scale = np.exp2(byte - 127.0)
    codes = (blocks / scale).astype(np.float32).astype(dtype).astype(np.float64)
    return np.moveaxis((codes * scale).reshape(v.shape), -1, axis)


WIDE = False


def mx_kscale(k):
    if not WIDE:
        return np.ones(k)
    levels = np.array([10, -10, 5, -5, 0])
    a = np.random.permutation(np.resize(levels, k // 512 * 4)).reshape(k // 512, 4)
    idx = np.arange(k)
    return np.exp2(a[idx // 512, idx % 128 // 32])


BF16 = ml_dtypes.bfloat16


def bf(x):
    return np.asarray(x, np.float32).astype(BF16)


def f64(x):
    return np.asarray(x).astype(np.float64)


B, N, D = 16, 1024, 128


def sigmoid(u):
    return 1.0 / (1.0 + np.exp(-u))


def setup_inputs():
    a = np.log(mx_kscale(N))
    return {"q": bf(np.random.standard_normal((B, N, D))),
            "k": bf(np.random.standard_normal((B, N, D)) - a[None, :, None]),
            "v": bf(np.random.standard_normal((B, N, D)) * 0.125 * np.sqrt(N)),
            "bias": bf(np.random.standard_normal((N, N)) + a[None, :])}


def reference(q, k, v, bias):
    q, k, v, bias = f64(q), f64(k), f64(v), f64(bias)
    mb = bias.max(axis=1, keepdims=True)
    mk = k.max(axis=1, keepdims=True)
    eb = np.exp(bias - mb)
    ek = np.exp(k - mk)
    ebq = mxq(eb, 1, "e4m3")
    num = ebq @ mxq(ek * v, 1, "e4m3")
    den = ebq @ mxq(ek, 1, "e4m3")
    return sigmoid(q) * (num / den)

@@ -1,0 +1,345 @@
+from contextlib import ExitStack
+
+import concourse.mybir as mybir
+from concourse.masks import make_identity
+
+F32 = mybir.dt.float32
+BF16 = mybir.dt.bfloat16
+U32 = mybir.dt.uint32
+U8 = mybir.dt.uint8
+FP8X4 = mybir.dt.float8_e4m3fn_x4
+ACT = mybir.ActivationFunctionType
+ALU = mybir.AluOpType
+AX = mybir.AxisListType
+
+P = 128
+B = 16
+N = 1024
+D = 128
+FLOPS = 2 * 2 * B * N * N * D
+
+N_PAIRS = B // 2
+N_UNITS = 2 * N_PAIRS
+N_STEPS2 = 32
+
+
+def tile_modelnew_kernel(tc, q, k, v, bias, out):
+    nc = tc.nc
+    with ExitStack() as ctx:
+        keep = ctx.enter_context(tc.tile_pool(name="keep", bufs=1))
+        tpool = ctx.enter_context(tc.tile_pool(name="tpool", bufs=4))
+        psx = ctx.enter_context(tc.psum_pool(name="psx", bufs=4))
+        pst = ctx.enter_context(tc.psum_pool(name="pst", bufs=2))
+        psm = ctx.enter_context(tc.psum_pool(name="psm", bufs=1))
+        ctx.enter_context(tc.manual_schedule())
+
+        ident = keep.tile([P, P], BF16, name="ident", tag="ident")
+        ident4 = keep.tile([P, 4, P], BF16, name="ident4", tag="ident4")
+        negmb = keep.tile([P, 8], F32, name="negmb", tag="negmb")
+        eb_codes = keep.tile([P, 8, 256], U32, name="eb_codes", tag="eb_codes", align_bytes=64)
+        eb_scales = keep.tile([P, 8, 256], U8, name="eb_scales", tag="eb_scales", align_bytes=64)
+        x_codes = keep.tile([P, 4, 2, 2, 512], U32, name="x_codes", tag="x_codes", align_bytes=64)
+        x_scales = keep.tile([P, 4, 2, 2, 512], U8, name="x_scales", tag="x_scales", align_bytes=64)
+        e_all = keep.tile([P, B, N], F32, name="e_all", tag="e_all")
+
+        make_identity(nc, ident[:])
+        nc.vector.tensor_copy(out=ident4[:], in_=ident[:].unsqueeze(1).to_broadcast([P, 4, P]))
+
+        kts = {}
+        vts = {}
+        qts = {}
+        mkt = {}
+        negmk = {}
+        xbs = {}
+        xfs = {}
+        ekfs = {}
+        grps = {}
+        ebps = {}
+        ebts = {}
+        ebgs = {}
+        dens = {}
+        nums = {}
+        tts = {}
+        osts = {}
+
+        def on_vector(pi, bi):
+            return pi % 2 == 1 and bi == 1
+
+        def mx(s):
+            quad, m = divmod(s, 8)
+            if s % 3 < 2:
+                den = pst.tile([P, 512], F32, name="den", tag="tr")
+            else:
+                den = psm.tile([P, 512], F32, name="den", tag="mxa")
+            if s % 5 < 4:
+                num = psx.tile([P, 512], F32, name="num", tag="x")
+            else:
+                num = psm.tile([P, 512], F32, name="num", tag="mxb")
+            dens[s] = den
+            nums[s] = num
+            for bank, kind in ((den, 1), (num, 0)):
+                for c in range(2):
+                    nc.tensor.matmul_mx(
+                        out=bank[:],
+                        lhsT=eb_codes[:, m, 128 * c : 128 * c + 128].bitcast(FP8X4),
+                        lhsT_scale=eb_scales[:, m, 128 * c : 128 * c + 128],
+                        rhs=x_codes[:, quad, c, kind, :].bitcast(FP8X4),
+                        rhs_scale=x_scales[:, quad, c, kind, :],
+                        start=(c == 0),
+                        stop=(c == 1),
+                    )
+
+        def tstep(s):
+            quad, m = divmod(s, 8)
+            tt = tpool.tile([P, 4, D], F32, name="tt", tag="tt")
+            tts[s] = tt
+            nc.vector.scalar_tensor_tensor(
+                out=tt[:],
+                in0=e_all[:, 4 * quad : 4 * quad + 4, D * m : D * m + D],
+                scalar=1.0,
+                in1=dens[s][:].rearrange("p (b d) -> p b d", b=4),
+                op0=ALU.add,
+                op1=ALU.mult,
+            )
+
+        def sstep(s):
+            tt = tts[s]
+            nc.scalar.activation(out=tt[:], in_=tt[:], func=ACT.Abs_reciprocal_sqrt)
+            nc.scalar.activation(out=tt[:], in_=tt[:], func=ACT.Square)
+
+        with ExitStack() as ph1:
+            ld = ph1.enter_context(tc.tile_pool(name="ld", bufs=3))
+            wk = ph1.enter_context(tc.tile_pool(name="wk", bufs=2))
+
+            bias_sb = wk.tile([P, 8, N], BF16, name="bias_sb", tag="bias_sb", bufs=1)
+            bias_v = bias.rearrange("(p m) j -> p m j", m=8)
+
+            def load_k(pi):
+                kt = ld.tile([P, 2, 2, 512], BF16, name="kt", tag="kt")
+                kts[pi] = kt
+                nc.sync.dma_start(
+                    out=kt[:],
+                    in_=k[2 * pi : 2 * pi + 2].rearrange("b (c p t) d -> p b c (t d)", c=2, p=P, t=4),
+                )
+
+            def load_v(pi):
+                vt = ld.tile([P, 2, 2, 512], BF16, name="vt", tag="vt")
+                vts[pi] = vt
+                nc.sync.dma_start(
+                    out=vt[:],
+                    in_=v[2 * pi : 2 * pi + 2].rearrange("b (c p t) d -> p b c (t d)", c=2, p=P, t=4),
+                )
+
+            def load_q(pi):
+                qt = ld.tile([P, 2, N], BF16, name="qt", tag="qt", bufs=2)
+                qts[pi] = qt
+                nc.sync.dma_start(
+                    out=qt[:], in_=q[2 * pi : 2 * pi + 2].rearrange("b (p m) d -> p b (m d)", m=8)
+                )
+
+            def load_bias(h):
+                nc.sync.dma_start(out=bias_sb[:, 4 * h : 4 * h + 4, :], in_=bias_v[:, 4 * h : 4 * h + 4, :])
+
+            def tree(pi):
+                kt = kts[pi]
+                m1 = wk.tile([P, 2, 512], BF16, name="m1", tag="m1")
+                nc.vector.tensor_tensor(out=m1[:], in0=kt[:, :, 0, :], in1=kt[:, :, 1, :], op=ALU.max)
+                m2 = wk.tile([P, 2, 256], BF16, name="m2", tag="m2")
+                nc.vector.tensor_tensor(out=m2[:], in0=m1[:, :, 0:256], in1=m1[:, :, 256:512], op=ALU.max)
+                m3 = wk.tile([P, 2, 128], BF16, name="m3", tag="m3")
+                nc.vector.tensor_tensor(out=m3[:], in0=m2[:, :, 0:128], in1=m2[:, :, 128:256], op=ALU.max)
+                tb = pst.tile([P, 2, P], BF16, name="mkt", tag="tr")
+                mkt[pi] = tb
+                for bi in range(2):
+                    nc.tensor.transpose(tb[:, bi, :], m3[:, bi, :], ident[:])
+
+            def reduce_mk(pi):
+                nm = wk.tile([P, 2], BF16, name="negmk", tag="negmk", bufs=3)
+                negmk[pi] = nm
+                with nc.allow_low_precision(reason="the maximum of bfloat16 values is a bfloat16 value"):
+                    nc.vector.tensor_reduce(out=nm[:], in_=mkt[pi][:], axis=AX.X, op=ALU.max, negate=True)
+                if on_vector(pi, 1):
+                    nb = psx.tile([P, D], F32, name="nb", tag="x")
+                    nc.tensor.matmul(
+                        nb[:], lhsT=nm[:, 1:2].to_broadcast([P, P]), rhs=ident[:], start=True, stop=True
+                    )
+                    xf = wk.tile([P, 2, D, 4], F32, name="xf", tag="xf")
+                    xfs[pi] = xf
+                    nc.vector.tensor_tensor(
+                        out=xf[:],
+                        in0=kts[pi][:, 1, :, :].rearrange("p c (t d) -> p c d t", t=4),
+                        in1=nb[:].unsqueeze(1).unsqueeze(3).to_broadcast([P, 2, D, 4]),
+                        op=ALU.add,
+                    )
+
+            def sub(u):
+                pi, c = divmod(u, 2)
+                for bi in range(2):
+                    if on_vector(pi, bi):
+                        continue
+                    xb = psx.tile([P, 512], F32, name="xb", tag="x")
+                    xbs[(u, bi)] = xb
+                    nc.tensor.matmul(
+                        xb[:],
+                        lhsT=negmk[pi][:, bi : bi + 1].to_broadcast([P, P]),
+                        rhs=ident4[:].rearrange("p t d -> p (t d)"),
+                        start=True,
+                        stop=False,
+                    )
+                    nc.tensor.matmul(xb[:], lhsT=ident[:], rhs=kts[pi][:, bi, c, :], start=False, stop=True)
+
+            def exps(u):
+                pi, c = divmod(u, 2)
+                ef = wk.tile([P, 2, D, 4], F32, name="ekf", tag="ekf", bufs=3)
+                ekfs[u] = ef
+                for bi in range(2):
+                    if on_vector(pi, bi):
+                        src = xfs[pi][:, c, :, :]
+                    else:
+                        src = xbs[(u, bi)][:].rearrange("p (t d) -> p d t", t=4)
+                    nc.scalar.activation(out=ef[:, bi, :, :], in_=src, func=ACT.Exp)
+
+            def ve(u):
+                pi, c = divmod(u, 2)
+                ef = ekfs[u]
+                g = wk.tile([P, 2, 2, 512], BF16, name="grp", tag="grp", bufs=3, align_bytes=64)
+                grps[u] = g
+                nc.vector.tensor_copy(out=g[:, 1, :, :], in_=ef[:].rearrange("p b d t -> p b (d t)"))
+                nc.vector.tensor_tensor(
+                    out=g[:, 0, :, :].rearrange("p b (d t) -> p b d t", t=4),
+                    in0=ef[:],
+                    in1=vts[pi][:, :, c, :].rearrange("p b (t d) -> p b d t", t=4),
+                    op=ALU.mult,
+                )
+
+            def qz(u):
+                pi, c = divmod(u, 2)
+                quad, h = divmod(pi, 2)
+                g = grps[u]
+                for kind in range(2):
+                    nc.vector.quantize_mx(
+                        out=x_codes[:, quad, c, kind, 256 * h : 256 * h + 256].bitcast(FP8X4),
+                        scales=x_scales[:, quad, c, kind, 256 * h : 256 * h + 256],
+                        in_=g[:, kind, :, :].rearrange("p b x -> p (b x)"),
+                    )
+
+            def eq(b):
+                nc.scalar.activation(out=e_all[:, b, :], in_=qts[b // 2][:, b % 2, :], func=ACT.Exp, scale=-1.0)
+
+            def bias_max(h):
+                sl = slice(4 * h, 4 * h + 4)
+                b1 = wk.tile([P, 4, 512], BF16, name="b1", tag="b1", bufs=1)
+                nc.vector.tensor_tensor(out=b1[:], in0=bias_sb[:, sl, 0:512], in1=bias_sb[:, sl, 512:1024], op=ALU.max)
+                b2 = wk.tile([P, 4, 256], BF16, name="b2", tag="b2", bufs=1)
+                nc.vector.tensor_tensor(out=b2[:], in0=b1[:, :, 0:256], in1=b1[:, :, 256:512], op=ALU.max)
+                b3 = wk.tile([P, 4, 128], BF16, name="b3", tag="b3", bufs=1)
+                nc.vector.tensor_tensor(out=b3[:], in0=b2[:, :, 0:128], in1=b2[:, :, 128:256], op=ALU.max)
+                nc.vector.tensor_reduce(out=negmb[:, sl], in_=b3[:], axis=AX.X, op=ALU.max, negate=True)
+
+            def eb_exp(m):
+                ebp = wk.tile([P, 2, 4, P], BF16, name="ebp", tag="ebp")
+                ebps[m] = ebp
+                nc.scalar.activation(
+                    out=ebp[:],
+                    in_=bias_sb[:, m, :].rearrange("p (c j t) -> p c t j", c=2, t=4),
+                    func=ACT.Exp,
+                    bias=negmb[:, m : m + 1],
+                    scale=1.0,
+                )
+                ebt = pst.tile([P, 2, 4, P], BF16, name="ebt", tag="tr")
+                ebts[m] = ebt
+                for c in range(2):
+                    for t in range(4):
+                        nc.tensor.transpose(ebt[:, c, t, :], ebp[:, c, t, :], ident[:])
+
+            def eb_out(m):
+                ebg = wk.tile([P, 2, P, 4], BF16, name="ebg", tag="ebg", align_bytes=64)
+                ebgs[m] = ebg
+                nc.scalar.copy(out=ebg[:], in_=ebts[m][:].rearrange("p c t i -> p c i t"))
+
+            def eb_qz(m):
+                nc.vector.quantize_mx(
+                    out=eb_codes[:, m, :].bitcast(FP8X4),
+                    scales=eb_scales[:, m, :],
+                    in_=ebgs[m][:].rearrange("p c i t -> p (c i t)"),
+                )
+
+            load_k(0)
+            load_q(0)
+            load_bias(0)
+            load_v(0)
+            load_k(1)
+            load_bias(1)
+            tree(0)
+            eq(0)
+            reduce_mk(0)
+            sub(0)
+            bias_max(0)
+
+            for step in range(N_UNITS):
+                pi, c = divmod(step, 2)
+                if c == 0:
+                    if pi + 2 < N_PAIRS:
+                        load_k(pi + 2)
+                    if pi + 1 < N_PAIRS:
+                        load_q(pi + 1)
+                        load_v(pi + 1)
+                if step >= 1:
+                    ve(step - 1)
+                if c == 1 and pi + 1 < N_PAIRS:
+                    reduce_mk(pi + 1)
+                if step + 1 < N_UNITS:
+                    sub(step + 1)
+                exps(step)
+                if step >= 2:
+                    qz(step - 2)
+                if step + 1 < B:
+                    eq(step + 1)
+                if c == 0:
+                    if pi >= 1:
+                        eb_qz(pi - 1)
+                    if pi + 1 < N_PAIRS:
+                        tree(pi + 1)
+                    eb_exp(pi)
+                else:
+                    eb_out(pi)
+                if step == 4:
+                    bias_max(1)
+
+            mx(0)
+            mx(1)
+            tstep(0)
+            tstep(1)
+            sstep(0)
+            sstep(1)
+            ve(N_UNITS - 1)
+            eb_qz(7)
+            qz(N_UNITS - 2)
+            qz(N_UNITS - 1)
+
+        with tc.tile_pool(name="ost", bufs=3) as opool:
+
+            def fin(s):
+                quad, m = divmod(s, 8)
+                if m % 4 == 0:
+                    osts[s // 4] = opool.tile([P, 4, 4, D], F32, name="ost", tag="ost")
+                ost = osts[s // 4]
+                nc.vector.tensor_tensor(
+                    out=ost[:, :, m % 4, :],
+                    in0=nums[s][:].rearrange("p (b d) -> p b d", b=4),
+                    in1=tts[s][:],
+                    op=ALU.mult,
+                )
+                if m % 4 == 3:
+                    m0 = m - 3
+                    nc.sync.dma_start(
+                        out=out[4 * quad : 4 * quad + 4].rearrange("b (p m) d -> p b m d", m=8)[:, :, m0 : m0 + 4, :],
+                        in_=ost[:],
+                    )
+
+            for s in range(2, N_STEPS2 + 2):
+                if s < N_STEPS2:
+                    mx(s)
+                    tstep(s)
+                    sstep(s)
+                fin(s - 2)

@@ -21,13 +21,15 @@ FLOPS = 2 * 2 * B * N * N * D
 N_PAIRS = B // 2
 N_UNITS = 2 * N_PAIRS
 N_STEPS2 = 32
+D_ON_SCALAR = ()
+MX0_STEP = 13
 
 
 def tile_modelnew_kernel(tc, q, k, v, bias, out):
     nc = tc.nc
     with ExitStack() as ctx:
         keep = ctx.enter_context(tc.tile_pool(name="keep", bufs=1))
-        tpool = ctx.enter_context(tc.tile_pool(name="tpool", bufs=4))
+        tpool = ctx.enter_context(tc.tile_pool(name="tpool", bufs=6))
         psx = ctx.enter_context(tc.psum_pool(name="psx", bufs=4))
         pst = ctx.enter_context(tc.psum_pool(name="pst", bufs=2))
         psm = ctx.enter_context(tc.psum_pool(name="psm", bufs=1))
@@ -49,6 +51,9 @@ def tile_modelnew_kernel(tc, q, k, v, bias, out):
         vts = {}
         qts = {}
         mkt = {}
+        trees = {}
+        nbs = {}
+        bms = {}
         negmk = {}
         xbs = {}
         xfs = {}
@@ -67,14 +72,14 @@ def tile_modelnew_kernel(tc, q, k, v, bias, out):
 
         def mx(s):
             quad, m = divmod(s, 8)
-            if s % 3 < 2:
-                den = pst.tile([P, 512], F32, name="den", tag="tr")
-            else:
+            if s % 3 == 0:
                 den = psm.tile([P, 512], F32, name="den", tag="mxa")
-            if s % 5 < 4:
-                num = psx.tile([P, 512], F32, name="num", tag="x")
             else:
+                den = pst.tile([P, 512], F32, name="den", tag="tr")
+            if s % 5 == 0:
                 num = psm.tile([P, 512], F32, name="num", tag="mxb")
+            else:
+                num = psx.tile([P, 512], F32, name="num", tag="x")
             dens[s] = den
             nums[s] = num
             for bank, kind in ((den, 1), (num, 0)):
@@ -102,10 +107,11 @@ def tile_modelnew_kernel(tc, q, k, v, bias, out):
                 op1=ALU.mult,
             )
 
-        def sstep(s):
-            tt = tts[s]
-            nc.scalar.activation(out=tt[:], in_=tt[:], func=ACT.Abs_reciprocal_sqrt)
-            nc.scalar.activation(out=tt[:], in_=tt[:], func=ACT.Square)
+        def ars(s):
+            nc.scalar.activation(out=tts[s][:], in_=tts[s][:], func=ACT.Abs_reciprocal_sqrt)
+
+        def square(s):
+            nc.scalar.activation(out=tts[s][:], in_=tts[s][:], func=ACT.Square)
 
         with ExitStack() as ph1:
             ld = ph1.enter_context(tc.tile_pool(name="ld", bufs=3))
@@ -140,12 +146,19 @@ def tile_modelnew_kernel(tc, q, k, v, bias, out):
             def load_bias(h):
                 nc.sync.dma_start(out=bias_sb[:, 4 * h : 4 * h + 4, :], in_=bias_v[:, 4 * h : 4 * h + 4, :])
 
-            def tree(pi):
-                kt = kts[pi]
+            def tree1(pi):
                 m1 = wk.tile([P, 2, 512], BF16, name="m1", tag="m1")
-                nc.vector.tensor_tensor(out=m1[:], in0=kt[:, :, 0, :], in1=kt[:, :, 1, :], op=ALU.max)
+                trees[(pi, 1)] = m1
+                nc.vector.tensor_tensor(out=m1[:], in0=kts[pi][:, :, 0, :], in1=kts[pi][:, :, 1, :], op=ALU.max)
+
+            def tree2(pi):
+                m1 = trees[(pi, 1)]
                 m2 = wk.tile([P, 2, 256], BF16, name="m2", tag="m2")
+                trees[(pi, 2)] = m2
                 nc.vector.tensor_tensor(out=m2[:], in0=m1[:, :, 0:256], in1=m1[:, :, 256:512], op=ALU.max)
+
+            def tree3(pi):
+                m2 = trees[(pi, 2)]
                 m3 = wk.tile([P, 2, 128], BF16, name="m3", tag="m3")
                 nc.vector.tensor_tensor(out=m3[:], in0=m2[:, :, 0:128], in1=m2[:, :, 128:256], op=ALU.max)
                 tb = pst.tile([P, 2, P], BF16, name="mkt", tag="tr")
@@ -160,17 +173,20 @@ def tile_modelnew_kernel(tc, q, k, v, bias, out):
                     nc.vector.tensor_reduce(out=nm[:], in_=mkt[pi][:], axis=AX.X, op=ALU.max, negate=True)
                 if on_vector(pi, 1):
                     nb = psx.tile([P, D], F32, name="nb", tag="x")
+                    nbs[pi] = nb
                     nc.tensor.matmul(
                         nb[:], lhsT=nm[:, 1:2].to_broadcast([P, P]), rhs=ident[:], start=True, stop=True
                     )
-                    xf = wk.tile([P, 2, D, 4], F32, name="xf", tag="xf")
-                    xfs[pi] = xf
-                    nc.vector.tensor_tensor(
-                        out=xf[:],
-                        in0=kts[pi][:, 1, :, :].rearrange("p c (t d) -> p c d t", t=4),
-                        in1=nb[:].unsqueeze(1).unsqueeze(3).to_broadcast([P, 2, D, 4]),
-                        op=ALU.add,
-                    )
+
+            def sub_on_vector(pi):
+                xf = wk.tile([P, 2, D, 4], F32, name="xf", tag="xf")
+                xfs[pi] = xf
+                nc.vector.tensor_tensor(
+                    out=xf[:],
+                    in0=kts[pi][:, 1, :, :].rearrange("p c (t d) -> p c d t", t=4),
+                    in1=nbs[pi][:].unsqueeze(1).unsqueeze(3).to_broadcast([P, 2, D, 4]),
+                    op=ALU.add,
+                )
 
             def sub(u):
                 pi, c = divmod(u, 2)
@@ -188,26 +204,34 @@ def tile_modelnew_kernel(tc, q, k, v, bias, out):
                     )
                     nc.tensor.matmul(xb[:], lhsT=ident[:], rhs=kts[pi][:, bi, c, :], start=False, stop=True)
 
-            def exps(u):
+            def exp_src(u, bi):
                 pi, c = divmod(u, 2)
+                if on_vector(pi, bi):
+                    return xfs[pi][:, c, :, :]
+                return xbs[(u, bi)][:].rearrange("p (t d) -> p d t", t=4)
+
+            def exps(u):
                 ef = wk.tile([P, 2, D, 4], F32, name="ekf", tag="ekf", bufs=3)
                 ekfs[u] = ef
-                for bi in range(2):
-                    if on_vector(pi, bi):
-                        src = xfs[pi][:, c, :, :]
-                    else:
-                        src = xbs[(u, bi)][:].rearrange("p (t d) -> p d t", t=4)
-                    nc.scalar.activation(out=ef[:, bi, :, :], in_=src, func=ACT.Exp)
-
-            def ve(u):
-                pi, c = divmod(u, 2)
-                ef = ekfs[u]
                 g = wk.tile([P, 2, 2, 512], BF16, name="grp", tag="grp", bufs=3, align_bytes=64)
                 grps[u] = g
-                nc.vector.tensor_copy(out=g[:, 1, :, :], in_=ef[:].rearrange("p b d t -> p b (d t)"))
+                for bi in range(2):
+                    nc.scalar.activation(out=ef[:, bi, :, :], in_=exp_src(u, bi), func=ACT.Exp)
+                if u in D_ON_SCALAR:
+                    for bi in range(2):
+                        nc.scalar.activation(
+                            out=g[:, 1, bi, :].rearrange("p (d t) -> p d t", t=4), in_=exp_src(u, bi), func=ACT.Exp
+                        )
+
+            def cast_ek(u):
+                if u not in D_ON_SCALAR:
+                    nc.vector.tensor_copy(out=grps[u][:, 1, :, :], in_=ekfs[u][:].rearrange("p b d t -> p b (d t)"))
+
+            def mul_v(u):
+                pi, c = divmod(u, 2)
                 nc.vector.tensor_tensor(
-                    out=g[:, 0, :, :].rearrange("p b (d t) -> p b d t", t=4),
-                    in0=ef[:],
+                    out=grps[u][:, 0, :, :].rearrange("p b (d t) -> p b d t", t=4),
+                    in0=ekfs[u][:],
                     in1=vts[pi][:, :, c, :].rearrange("p b (t d) -> p b d t", t=4),
                     op=ALU.mult,
                 )
@@ -226,15 +250,24 @@ def tile_modelnew_kernel(tc, q, k, v, bias, out):
             def eq(b):
                 nc.scalar.activation(out=e_all[:, b, :], in_=qts[b // 2][:, b % 2, :], func=ACT.Exp, scale=-1.0)
 
-            def bias_max(h):
+            def bias_max(h, level):
                 sl = slice(4 * h, 4 * h + 4)
-                b1 = wk.tile([P, 4, 512], BF16, name="b1", tag="b1", bufs=1)
-                nc.vector.tensor_tensor(out=b1[:], in0=bias_sb[:, sl, 0:512], in1=bias_sb[:, sl, 512:1024], op=ALU.max)
-                b2 = wk.tile([P, 4, 256], BF16, name="b2", tag="b2", bufs=1)
-                nc.vector.tensor_tensor(out=b2[:], in0=b1[:, :, 0:256], in1=b1[:, :, 256:512], op=ALU.max)
-                b3 = wk.tile([P, 4, 128], BF16, name="b3", tag="b3", bufs=1)
-                nc.vector.tensor_tensor(out=b3[:], in0=b2[:, :, 0:128], in1=b2[:, :, 128:256], op=ALU.max)
-                nc.vector.tensor_reduce(out=negmb[:, sl], in_=b3[:], axis=AX.X, op=ALU.max, negate=True)
+                if level == 0:
+                    b1 = wk.tile([P, 4, 512], BF16, name="b1", tag="b1", bufs=1)
+                    bms[1] = b1
+                    nc.vector.tensor_tensor(
+                        out=b1[:], in0=bias_sb[:, sl, 0:512], in1=bias_sb[:, sl, 512:1024], op=ALU.max
+                    )
+                elif level == 1:
+                    b2 = wk.tile([P, 4, 256], BF16, name="b2", tag="b2", bufs=1)
+                    bms[2] = b2
+                    nc.vector.tensor_tensor(out=b2[:], in0=bms[1][:, :, 0:256], in1=bms[1][:, :, 256:512], op=ALU.max)
+                elif level == 2:
+                    b3 = wk.tile([P, 4, 128], BF16, name="b3", tag="b3", bufs=1)
+                    bms[3] = b3
+                    nc.vector.tensor_tensor(out=b3[:], in0=bms[2][:, :, 0:128], in1=bms[2][:, :, 128:256], op=ALU.max)
+                else:
+                    nc.vector.tensor_reduce(out=negmb[:, sl], in_=bms[3][:], axis=AX.X, op=ALU.max, negate=True)
 
             def eb_exp(m):
                 ebp = wk.tile([P, 2, 4, P], BF16, name="ebp", tag="ebp")
@@ -266,61 +299,89 @@ def tile_modelnew_kernel(tc, q, k, v, bias, out):
 
             load_k(0)
             load_q(0)
-            load_bias(0)
-            load_v(0)
             load_k(1)
+            load_v(0)
+            load_bias(0)
             load_bias(1)
-            tree(0)
+            tree1(0)
+            tree2(0)
+            tree3(0)
             eq(0)
             reduce_mk(0)
             sub(0)
-            bias_max(0)
 
             for step in range(N_UNITS):
                 pi, c = divmod(step, 2)
+                nxt = pi + 1
                 if c == 0:
                     if pi + 2 < N_PAIRS:
                         load_k(pi + 2)
-                    if pi + 1 < N_PAIRS:
-                        load_q(pi + 1)
-                        load_v(pi + 1)
-                if step >= 1:
-                    ve(step - 1)
-                if c == 1 and pi + 1 < N_PAIRS:
-                    reduce_mk(pi + 1)
+                    if nxt < N_PAIRS:
+                        load_q(nxt)
+                        load_v(nxt)
                 if step + 1 < N_UNITS:
                     sub(step + 1)
                 exps(step)
-                if step >= 2:
-                    qz(step - 2)
-                if step + 1 < B:
-                    eq(step + 1)
                 if c == 0:
-                    if pi >= 1:
-                        eb_qz(pi - 1)
-                    if pi + 1 < N_PAIRS:
-                        tree(pi + 1)
-                    eb_exp(pi)
+                    if pi >= 2:
+                        eb_out(pi - 2)
+                    eq(step + 1)
+                    if nxt < N_PAIRS:
+                        tree1(nxt)
+                    if step >= 1:
+                        cast_ek(step - 1)
+                    if nxt < N_PAIRS:
+                        tree2(nxt)
+                    if step >= 1:
+                        mul_v(step - 1)
+                    if nxt < N_PAIRS:
+                        tree3(nxt)
+                    if step >= 2:
+                        qz(step - 2)
+                    if pi in (1, 2):
+                        bias_max(pi - 1, 2)
+                    if nxt < N_PAIRS:
+                        reduce_mk(nxt)
+                    if pi in (1, 2):
+                        bias_max(pi - 1, 3)
                 else:
-                    eb_out(pi)
-                if step == 4:
-                    bias_max(1)
-
-            mx(0)
-            mx(1)
+                    if step + 1 < B:
+                        eq(step + 1)
+                    if pi >= 1:
+                        eb_exp(pi - 1)
+                    if pi in (0, 1):
+                        bias_max(pi, 0)
+                    cast_ek(step - 1)
+                    if pi in (0, 1):
+                        bias_max(pi, 1)
+                    mul_v(step - 1)
+                    if nxt < N_PAIRS and on_vector(nxt, 1):
+                        sub_on_vector(nxt)
+                    if step >= 2:
+                        qz(step - 2)
+                    if pi >= 2:
+                        eb_qz(pi - 2)
+                if step == MX0_STEP:
+                    mx(0)
             tstep(0)
-            tstep(1)
-            sstep(0)
-            sstep(1)
-            ve(N_UNITS - 1)
-            eb_qz(7)
+            eb_exp(7)
+            eb_out(6)
+            mx(1)
+            ars(0)
+            eb_out(7)
+            mx(2)
+            cast_ek(N_UNITS - 1)
+            mul_v(N_UNITS - 1)
+            eb_qz(6)
             qz(N_UNITS - 2)
             qz(N_UNITS - 1)
+            eb_qz(7)
 
         with tc.tile_pool(name="ost", bufs=3) as opool:
 
             def fin(s):
                 quad, m = divmod(s, 8)
+                out_v = out[4 * quad : 4 * quad + 4].rearrange("b (p m) d -> p b m d", m=8)
                 if m % 4 == 0:
                     osts[s // 4] = opool.tile([P, 4, 4, D], F32, name="ost", tag="ost")
                 ost = osts[s // 4]
@@ -330,16 +391,18 @@ def tile_modelnew_kernel(tc, q, k, v, bias, out):
                     in1=tts[s][:],
                     op=ALU.mult,
                 )
-                if m % 4 == 3:
-                    m0 = m - 3
-                    nc.sync.dma_start(
-                        out=out[4 * quad : 4 * quad + 4].rearrange("b (p m) d -> p b m d", m=8)[:, :, m0 : m0 + 4, :],
-                        in_=ost[:],
-                    )
+                if s >= N_STEPS2 - 4:
+                    nc.sync.dma_start(out=out_v[:, :, m : m + 1, :], in_=ost[:, :, m % 4 : m % 4 + 1, :])
+                elif m % 4 == 3:
+                    nc.sync.dma_start(out=out_v[:, :, m - 3 : m + 1, :], in_=ost[:])
 
-            for s in range(2, N_STEPS2 + 2):
-                if s < N_STEPS2:
+            for s in range(1, N_STEPS2 + 3):
+                if 3 <= s < N_STEPS2:
                     mx(s)
+                if s < N_STEPS2:
                     tstep(s)
-                    sstep(s)
-                fin(s - 2)
+                    ars(s)
+                if s - 1 < N_STEPS2:
+                    square(s - 1)
+                if s >= 3:
+                    fin(s - 3)

@@ -36,7 +36,7 @@ def tile_modelnew_kernel(tc, q, k, v, bias, out):
         ctx.enter_context(tc.manual_schedule())
 
         ident = keep.tile([P, P], BF16, name="ident", tag="ident")
-        ident4 = keep.tile([P, 4, P], BF16, name="ident4", tag="ident4")
+        ident_f = keep.tile([P, P], F32, name="ident_f", tag="ident_f")
         negmb = keep.tile([P, 8], F32, name="negmb", tag="negmb")
         eb_codes = keep.tile([P, 8, 256], U32, name="eb_codes", tag="eb_codes", align_bytes=64)
         eb_scales = keep.tile([P, 8, 256], U8, name="eb_scales", tag="eb_scales", align_bytes=64)
@@ -45,7 +45,7 @@ def tile_modelnew_kernel(tc, q, k, v, bias, out):
         e_all = keep.tile([P, B, N], F32, name="e_all", tag="e_all")
 
         make_identity(nc, ident[:])
-        nc.vector.tensor_copy(out=ident4[:], in_=ident[:].unsqueeze(1).to_broadcast([P, 4, P]))
+        make_identity(nc, ident_f[:])
 
         kts = {}
         vts = {}
@@ -59,7 +59,6 @@ def tile_modelnew_kernel(tc, q, k, v, bias, out):
         xfs = {}
         ekfs = {}
         grps = {}
-        ebps = {}
         ebts = {}
         ebgs = {}
         dens = {}
@@ -68,7 +67,7 @@ def tile_modelnew_kernel(tc, q, k, v, bias, out):
         osts = {}
 
         def on_vector(pi, bi):
-            return pi % 2 == 1 and bi == 1
+            return False
 
         def mx(s):
             quad, m = divmod(s, 8)
@@ -167,10 +166,9 @@ def tile_modelnew_kernel(tc, q, k, v, bias, out):
                     nc.tensor.transpose(tb[:, bi, :], m3[:, bi, :], ident[:])
 
             def reduce_mk(pi):
-                nm = wk.tile([P, 2], BF16, name="negmk", tag="negmk", bufs=3)
+                nm = wk.tile([P, 2], F32, name="negmk", tag="negmk", bufs=3)
                 negmk[pi] = nm
-                with nc.allow_low_precision(reason="the maximum of bfloat16 values is a bfloat16 value"):
-                    nc.vector.tensor_reduce(out=nm[:], in_=mkt[pi][:], axis=AX.X, op=ALU.max, negate=True)
+                nc.vector.tensor_reduce(out=nm[:], in_=mkt[pi][:], axis=AX.X, op=ALU.max, negate=True)
                 if on_vector(pi, 1):
                     nb = psx.tile([P, D], F32, name="nb", tag="x")
                     nbs[pi] = nb
@@ -195,13 +193,15 @@ def tile_modelnew_kernel(tc, q, k, v, bias, out):
                         continue
                     xb = psx.tile([P, 512], F32, name="xb", tag="x")
                     xbs[(u, bi)] = xb
-                    nc.tensor.matmul(
-                        xb[:],
-                        lhsT=negmk[pi][:, bi : bi + 1].to_broadcast([P, P]),
-                        rhs=ident4[:].rearrange("p t d -> p (t d)"),
-                        start=True,
-                        stop=False,
-                    )
+                    for t in range(4):
+                        nc.tensor.matmul(
+                            xb[:, D * t : D * t + D],
+                            lhsT=negmk[pi][:, bi : bi + 1].to_broadcast([P, P]),
+                            rhs=ident_f[:],
+                            is_transpose=True,
+                            start=(t == 0),
+                            stop=False,
+                        )
                     nc.tensor.matmul(xb[:], lhsT=ident[:], rhs=kts[pi][:, bi, c, :], start=False, stop=True)
 
             def exp_src(u, bi):
@@ -269,26 +269,38 @@ def tile_modelnew_kernel(tc, q, k, v, bias, out):
                 else:
                     nc.vector.tensor_reduce(out=negmb[:, sl], in_=bms[3][:], axis=AX.X, op=ALU.max, negate=True)
 
-            def eb_exp(m):
-                ebp = wk.tile([P, 2, 4, P], BF16, name="ebp", tag="ebp")
-                ebps[m] = ebp
-                nc.scalar.activation(
-                    out=ebp[:],
-                    in_=bias_sb[:, m, :].rearrange("p (c j t) -> p c t j", c=2, t=4),
-                    func=ACT.Exp,
-                    bias=negmb[:, m : m + 1],
-                    scale=1.0,
-                )
-                ebt = pst.tile([P, 2, 4, P], BF16, name="ebt", tag="tr")
-                ebts[m] = ebt
+            def eb_sub(m):
                 for c in range(2):
+                    if m < 6:
+                        ebt = psm.tile([P, 4, P], F32, name="ebt", tag="mxa" if c == 0 else "mxb")
+                    else:
+                        ebt = pst.tile([P, 4, P], F32, name="ebt", tag="tr")
+                    ebts[(m, c)] = ebt
                     for t in range(4):
-                        nc.tensor.transpose(ebt[:, c, t, :], ebp[:, c, t, :], ident[:])
+                        nc.tensor.matmul(
+                            ebt[:, t, :],
+                            lhsT=negmb[:, m : m + 1].to_broadcast([P, P]),
+                            rhs=ident_f[:],
+                            is_transpose=True,
+                            start=(t == 0),
+                            stop=False,
+                        )
+                    for t in range(4):
+                        nc.tensor.matmul(
+                            ebt[:, t, :],
+                            lhsT=bias_sb[:, m, 512 * c + t : 512 * c + 512 : 4],
+                            rhs=ident[:],
+                            start=False,
+                            stop=(t == 3),
+                        )
 
-            def eb_out(m):
+            def eb_exp(m):
                 ebg = wk.tile([P, 2, P, 4], BF16, name="ebg", tag="ebg", align_bytes=64)
                 ebgs[m] = ebg
-                nc.scalar.copy(out=ebg[:], in_=ebts[m][:].rearrange("p c t i -> p c i t"))
+                for c in range(2):
+                    nc.scalar.activation(
+                        out=ebg[:, c, :, :], in_=ebts[(m, c)][:].rearrange("p t i -> p i t"), func=ACT.Exp
+                    )
 
             def eb_qz(m):
                 nc.vector.quantize_mx(
@@ -319,12 +331,12 @@ def tile_modelnew_kernel(tc, q, k, v, bias, out):
                     if nxt < N_PAIRS:
                         load_q(nxt)
                         load_v(nxt)
+                if c == 1 and pi >= 1:
+                    eb_sub(pi - 1)
                 if step + 1 < N_UNITS:
                     sub(step + 1)
                 exps(step)
                 if c == 0:
-                    if pi >= 2:
-                        eb_out(pi - 2)
                     eq(step + 1)
                     if nxt < N_PAIRS:
                         tree1(nxt)
@@ -364,11 +376,10 @@ def tile_modelnew_kernel(tc, q, k, v, bias, out):
                 if step == MX0_STEP:
                     mx(0)
             tstep(0)
+            eb_sub(7)
             eb_exp(7)
-            eb_out(6)
             mx(1)
             ars(0)
-            eb_out(7)
             mx(2)
             cast_ek(N_UNITS - 1)
             mul_v(N_UNITS - 1)

@@ -21,7 +21,7 @@ FLOPS = 2 * 2 * B * N * N * D
 N_PAIRS = B // 2
 N_UNITS = 2 * N_PAIRS
 N_STEPS2 = 32
-D_ON_SCALAR = ()
+D_ON_SCALAR = (1, 5, 9, 13)
 MX0_STEP = 13
 
 

@@ -110,7 +110,10 @@ def tile_modelnew_kernel(tc, q, k, v, bias, out):
             nc.scalar.activation(out=tts[s][:], in_=tts[s][:], func=ACT.Abs_reciprocal_sqrt)
 
         def square(s):
-            nc.scalar.activation(out=tts[s][:], in_=tts[s][:], func=ACT.Square)
+            if s % 8 == 3:
+                nc.gpsimd.tensor_tensor(out=tts[s][:], in0=tts[s][:], in1=tts[s][:], op=ALU.mult)
+            else:
+                nc.scalar.activation(out=tts[s][:], in_=tts[s][:], func=ACT.Square)
 
         with ExitStack() as ph1:
             ld = ph1.enter_context(tc.tile_pool(name="ld", bufs=3))
@@ -321,6 +324,10 @@ def tile_modelnew_kernel(tc, q, k, v, bias, out):
             eq(0)
             reduce_mk(0)
             sub(0)
+            tree1(1)
+            tree2(1)
+            tree3(1)
+            reduce_mk(1)
 
             for step in range(N_UNITS):
                 pi, c = divmod(step, 2)
@@ -338,21 +345,21 @@ def tile_modelnew_kernel(tc, q, k, v, bias, out):
                 exps(step)
                 if c == 0:
                     eq(step + 1)
-                    if nxt < N_PAIRS:
+                    if 2 <= nxt < N_PAIRS:
                         tree1(nxt)
                     if step >= 1:
                         cast_ek(step - 1)
-                    if nxt < N_PAIRS:
+                    if 2 <= nxt < N_PAIRS:
                         tree2(nxt)
                     if step >= 1:
                         mul_v(step - 1)
-                    if nxt < N_PAIRS:
+                    if 2 <= nxt < N_PAIRS:
                         tree3(nxt)
                     if step >= 2:
                         qz(step - 2)
                     if pi in (1, 2):
                         bias_max(pi - 1, 2)
-                    if nxt < N_PAIRS:
+                    if 2 <= nxt < N_PAIRS:
                         reduce_mk(nxt)
                     if pi in (1, 2):
                         bias_max(pi - 1, 3)
@@ -402,7 +409,7 @@ def tile_modelnew_kernel(tc, q, k, v, bias, out):
                     in1=tts[s][:],
                     op=ALU.mult,
                 )
-                if s >= N_STEPS2 - 4:
+                if s >= N_STEPS2 - 8:
                     nc.sync.dma_start(out=out_v[:, :, m : m + 1, :], in_=ost[:, :, m % 4 : m % 4 + 1, :])
                 elif m % 4 == 3:
                     nc.sync.dma_start(out=out_v[:, :, m - 3 : m + 1, :], in_=ost[:])

@@ -20,20 +20,34 @@ FLOPS = 2 * 2 * B * N * N * D
 
 N_PAIRS = B // 2
 N_UNITS = 2 * N_PAIRS
-N_STEPS2 = 32
-D_ON_SCALAR = (1, 5, 9, 13)
-MX0_STEP = 13
+HALF = N // 2
+TREE_LEAD = 3
+R_FIRST = 8
+TWO_MULS = ()
+EB_STEP = 8
+FIN_LAG = 3
+SINGLE = 4
 
 
 def tile_modelnew_kernel(tc, q, k, v, bias, out):
     nc = tc.nc
     with ExitStack() as ctx:
         keep = ctx.enter_context(tc.tile_pool(name="keep", bufs=1))
-        tpool = ctx.enter_context(tc.tile_pool(name="tpool", bufs=6))
+        tpool = ctx.enter_context(tc.tile_pool(name="tpool", bufs=8))
+        kpool = ctx.enter_context(tc.tile_pool(name="kpool", bufs=5))
         psx = ctx.enter_context(tc.psum_pool(name="psx", bufs=4))
         pst = ctx.enter_context(tc.psum_pool(name="pst", bufs=2))
         psm = ctx.enter_context(tc.psum_pool(name="psm", bufs=1))
-        ctx.enter_context(tc.manual_schedule())
+        ctx.enter_context(
+            tc.manual_schedule(
+                engines={
+                    mybir.EngineType.DVE,
+                    mybir.EngineType.Activation,
+                    mybir.EngineType.SP,
+                    mybir.EngineType.Pool,
+                }
+            )
+        )
 
         ident = keep.tile([P, P], BF16, name="ident", tag="ident")
         ident_f = keep.tile([P, P], F32, name="ident_f", tag="ident_f")
@@ -52,68 +66,86 @@ def tile_modelnew_kernel(tc, q, k, v, bias, out):
         qts = {}
         mkt = {}
         trees = {}
-        nbs = {}
         bms = {}
         negmk = {}
         xbs = {}
-        xfs = {}
         ekfs = {}
         grps = {}
         ebts = {}
         ebgs = {}
-        dens = {}
-        nums = {}
-        tts = {}
+        banks = {}
+        ats = {}
         osts = {}
+        done = {}
+        counts = {"den": 0, "num": 0}
 
-        def on_vector(pi, bi):
-            return False
+        def place(tile):
+            kind, i = tile
+            quad, r = divmod(i, 4)
+            return quad, (r if kind == "R" else 4 + r)
 
-        def mx(s):
-            quad, m = divmod(s, 8)
-            if s % 3 == 0:
-                den = psm.tile([P, 512], F32, name="den", tag="mxa")
+        def gate(tile):
+            quad, m = place(tile)
+            return e_all[:, 4 * quad : 4 * quad + 4, D * m : D * m + D]
+
+        def mx(tile, which):
+            quad, m = place(tile)
+            if tile[0] == "R" and which == "den":
+                bank = pst.tile([P, 512], F32, name="for_scalar", tag="tr")
             else:
-                den = pst.tile([P, 512], F32, name="den", tag="tr")
-            if s % 5 == 0:
-                num = psm.tile([P, 512], F32, name="num", tag="mxb")
-            else:
-                num = psx.tile([P, 512], F32, name="num", tag="x")
-            dens[s] = den
-            nums[s] = num
-            for bank, kind in ((den, 1), (num, 0)):
-                for c in range(2):
-                    nc.tensor.matmul_mx(
-                        out=bank[:],
-                        lhsT=eb_codes[:, m, 128 * c : 128 * c + 128].bitcast(FP8X4),
-                        lhsT_scale=eb_scales[:, m, 128 * c : 128 * c + 128],
-                        rhs=x_codes[:, quad, c, kind, :].bitcast(FP8X4),
-                        rhs_scale=x_scales[:, quad, c, kind, :],
-                        start=(c == 0),
-                        stop=(c == 1),
-                    )
+                cnt = counts["den"]
+                counts["den"] = cnt + 1
+                if cnt % 6 == 4:
+                    bank = psm.tile([P, 512], F32, name="for_vector", tag="mxa")
+                elif cnt % 6 == 5:
+                    bank = psm.tile([P, 512], F32, name="for_vector", tag="mxb")
+                else:
+                    bank = psx.tile([P, 512], F32, name="for_vector", tag="x")
+            banks[(tile, which)] = bank
+            kind = 1 if which == "den" else 0
+            for c in range(2):
+                nc.tensor.matmul_mx(
+                    out=bank[:],
+                    lhsT=eb_codes[:, m, 128 * c : 128 * c + 128].bitcast(FP8X4),
+                    lhsT_scale=eb_scales[:, m, 128 * c : 128 * c + 128],
+                    rhs=x_codes[:, quad, c, kind, :].bitcast(FP8X4),
+                    rhs_scale=x_scales[:, quad, c, kind, :],
+                    start=(c == 0),
+                    stop=(c == 1),
+                )
 
-        def tstep(s):
-            quad, m = divmod(s, 8)
-            tt = tpool.tile([P, 4, D], F32, name="tt", tag="tt")
-            tts[s] = tt
+        def first(tile):
+            bank = banks[(tile, "num" if tile[0] == "R" else "den")]
             nc.vector.scalar_tensor_tensor(
-                out=tt[:],
-                in0=e_all[:, 4 * quad : 4 * quad + 4, D * m : D * m + D],
+                out=gate(tile),
+                in0=gate(tile),
                 scalar=1.0,
-                in1=dens[s][:].rearrange("p (b d) -> p b d", b=4),
+                in1=bank[:].rearrange("p (b d) -> p b d", b=4),
                 op0=ALU.add,
                 op1=ALU.mult,
             )
 
-        def ars(s):
-            nc.scalar.activation(out=tts[s][:], in_=tts[s][:], func=ACT.Abs_reciprocal_sqrt)
-
-        def square(s):
-            if s % 8 == 3:
-                nc.gpsimd.tensor_tensor(out=tts[s][:], in0=tts[s][:], in1=tts[s][:], op=ALU.mult)
+        def ars(tile):
+            if tile[0] == "R":
+                at = kpool.tile([P, 4, D], F32, name="at", tag="at", bufs=10, offset=0)
+                ats[tile] = at
+                nc.scalar.activation(
+                    out=at[:],
+                    in_=banks[(tile, "den")][:].rearrange("p (b d) -> p b d", b=4),
+                    func=ACT.Abs_reciprocal_sqrt,
+                    scale=2.0,
+                )
             else:
-                nc.scalar.activation(out=tts[s][:], in_=tts[s][:], func=ACT.Square)
+                nc.scalar.activation(out=gate(tile), in_=gate(tile), func=ACT.Abs_reciprocal_sqrt)
+
+        def two_muls(tile):
+            return tile[0] == "R" and tile[1] % 4 in TWO_MULS
+
+        def square(tile):
+            if tile[0] == "P":
+                nc.scalar.activation(out=gate(tile), in_=gate(tile), func=ACT.Square)
+            elif not two_muls(tile):
+                nc.scalar.activation(out=ats[tile][:], in_=ats[tile][:], func=ACT.Square)
 
         with ExitStack() as ph1:
             ld = ph1.enter_context(tc.tile_pool(name="ld", bufs=3))
@@ -123,7 +155,7 @@ def tile_modelnew_kernel(tc, q, k, v, bias, out):
             bias_v = bias.rearrange("(p m) j -> p m j", m=8)
 
             def load_k(pi):
-                kt = ld.tile([P, 2, 2, 512], BF16, name="kt", tag="kt")
+                kt = kpool.tile([P, 2, 2, 512], BF16, name="kt", tag="kt", bufs=5, offset=0)
                 kts[pi] = kt
                 nc.sync.dma_start(
                     out=kt[:],
@@ -139,7 +171,7 @@ def tile_modelnew_kernel(tc, q, k, v, bias, out):
                 )
 
             def load_q(pi):
-                qt = ld.tile([P, 2, N], BF16, name="qt", tag="qt", bufs=2)
+                qt = ld.tile([P, 2, N], BF16, name="qt", tag="qt", bufs=3)
                 qts[pi] = qt
                 nc.sync.dma_start(
                     out=qt[:], in_=q[2 * pi : 2 * pi + 2].rearrange("b (p m) d -> p b (m d)", m=8)
@@ -161,39 +193,24 @@ def tile_modelnew_kernel(tc, q, k, v, bias, out):
 
             def tree3(pi):
                 m2 = trees[(pi, 2)]
-                m3 = wk.tile([P, 2, 128], BF16, name="m3", tag="m3")
+                m3 = wk.tile([P, 2, 128], BF16, name="m3", tag="m3", bufs=3)
+                trees[(pi, 3)] = m3
                 nc.vector.tensor_tensor(out=m3[:], in0=m2[:, :, 0:128], in1=m2[:, :, 128:256], op=ALU.max)
+
+            def turn_mk(pi):
                 tb = pst.tile([P, 2, P], BF16, name="mkt", tag="tr")
                 mkt[pi] = tb
                 for bi in range(2):
-                    nc.tensor.transpose(tb[:, bi, :], m3[:, bi, :], ident[:])
+                    nc.tensor.transpose(tb[:, bi, :], trees[(pi, 3)][:, bi, :], ident[:])
 
             def reduce_mk(pi):
-                nm = wk.tile([P, 2], F32, name="negmk", tag="negmk", bufs=3)
+                nm = wk.tile([P, 2], F32, name="negmk", tag="negmk", bufs=5)
                 negmk[pi] = nm
                 nc.vector.tensor_reduce(out=nm[:], in_=mkt[pi][:], axis=AX.X, op=ALU.max, negate=True)
-                if on_vector(pi, 1):
-                    nb = psx.tile([P, D], F32, name="nb", tag="x")
-                    nbs[pi] = nb
-                    nc.tensor.matmul(
-                        nb[:], lhsT=nm[:, 1:2].to_broadcast([P, P]), rhs=ident[:], start=True, stop=True
-                    )
-
-            def sub_on_vector(pi):
-                xf = wk.tile([P, 2, D, 4], F32, name="xf", tag="xf")
-                xfs[pi] = xf
-                nc.vector.tensor_tensor(
-                    out=xf[:],
-                    in0=kts[pi][:, 1, :, :].rearrange("p c (t d) -> p c d t", t=4),
-                    in1=nbs[pi][:].unsqueeze(1).unsqueeze(3).to_broadcast([P, 2, D, 4]),
-                    op=ALU.add,
-                )
 
             def sub(u):
                 pi, c = divmod(u, 2)
                 for bi in range(2):
-                    if on_vector(pi, bi):
-                        continue
                     xb = psx.tile([P, 512], F32, name="xb", tag="x")
                     xbs[(u, bi)] = xb
                     for t in range(4):
@@ -207,28 +224,18 @@ def tile_modelnew_kernel(tc, q, k, v, bias, out):
                         )
                     nc.tensor.matmul(xb[:], lhsT=ident[:], rhs=kts[pi][:, bi, c, :], start=False, stop=True)
 
-            def exp_src(u, bi):
-                pi, c = divmod(u, 2)
-                if on_vector(pi, bi):
-                    return xfs[pi][:, c, :, :]
-                return xbs[(u, bi)][:].rearrange("p (t d) -> p d t", t=4)
-
             def exps(u):
-                ef = wk.tile([P, 2, D, 4], F32, name="ekf", tag="ekf", bufs=3)
+                ef = wk.tile([P, 2, D, 4], F32, name="ekf", tag="ekf", bufs=5)
                 ekfs[u] = ef
-                g = wk.tile([P, 2, 2, 512], BF16, name="grp", tag="grp", bufs=3, align_bytes=64)
-                grps[u] = g
                 for bi in range(2):
-                    nc.scalar.activation(out=ef[:, bi, :, :], in_=exp_src(u, bi), func=ACT.Exp)
-                if u in D_ON_SCALAR:
-                    for bi in range(2):
-                        nc.scalar.activation(
-                            out=g[:, 1, bi, :].rearrange("p (d t) -> p d t", t=4), in_=exp_src(u, bi), func=ACT.Exp
-                        )
+                    nc.scalar.activation(
+                        out=ef[:, bi, :, :], in_=xbs[(u, bi)][:].rearrange("p (t d) -> p d t", t=4), func=ACT.Exp
+                    )
 
             def cast_ek(u):
-                if u not in D_ON_SCALAR:
-                    nc.vector.tensor_copy(out=grps[u][:, 1, :, :], in_=ekfs[u][:].rearrange("p b d t -> p b (d t)"))
+                g = wk.tile([P, 2, 2, 512], BF16, name="grp", tag="grp", bufs=3, align_bytes=64)
+                grps[u] = g
+                nc.vector.tensor_copy(out=g[:, 1, :, :], in_=ekfs[u][:].rearrange("p b d t -> p b (d t)"))
 
             def mul_v(u):
                 pi, c = divmod(u, 2)
@@ -251,7 +258,12 @@ def tile_modelnew_kernel(tc, q, k, v, bias, out):
                     )
 
             def eq(b):
-                nc.scalar.activation(out=e_all[:, b, :], in_=qts[b // 2][:, b % 2, :], func=ACT.Exp, scale=-1.0)
+                nc.scalar.activation(
+                    out=e_all[:, b, 0:HALF], in_=qts[b // 2][:, b % 2, 0:HALF], func=ACT.Tanh, scale=0.5
+                )
+                nc.scalar.activation(
+                    out=e_all[:, b, HALF:N], in_=qts[b // 2][:, b % 2, HALF:N], func=ACT.Exp, scale=-1.0
+                )
 
             def bias_max(h, level):
                 sl = slice(4 * h, 4 * h + 4)
@@ -274,10 +286,7 @@ def tile_modelnew_kernel(tc, q, k, v, bias, out):
 
             def eb_sub(m):
                 for c in range(2):
-                    if m < 6:
-                        ebt = psm.tile([P, 4, P], F32, name="ebt", tag="mxa" if c == 0 else "mxb")
-                    else:
-                        ebt = pst.tile([P, 4, P], F32, name="ebt", tag="tr")
+                    ebt = psm.tile([P, 4, P], F32, name="ebt", tag="mxa" if c == 0 else "mxb")
                     ebts[(m, c)] = ebt
                     for t in range(4):
                         nc.tensor.matmul(
@@ -298,7 +307,7 @@ def tile_modelnew_kernel(tc, q, k, v, bias, out):
                         )
 
             def eb_exp(m):
-                ebg = wk.tile([P, 2, P, 4], BF16, name="ebg", tag="ebg", align_bytes=64)
+                ebg = tpool.tile([P, 2, P, 4], BF16, name="ebg", tag="at", align_bytes=64)
                 ebgs[m] = ebg
                 for c in range(2):
                     nc.scalar.activation(
@@ -316,111 +325,171 @@ def tile_modelnew_kernel(tc, q, k, v, bias, out):
             load_q(0)
             load_k(1)
             load_v(0)
-            load_bias(0)
-            load_bias(1)
+            load_k(2)
+            load_q(1)
+            load_k(3)
             tree1(0)
             tree2(0)
             tree3(0)
+            turn_mk(0)
             eq(0)
             reduce_mk(0)
             sub(0)
             tree1(1)
             tree2(1)
             tree3(1)
+            turn_mk(1)
             reduce_mk(1)
+            tree1(2)
+            tree2(2)
+            tree3(2)
 
             for step in range(N_UNITS):
                 pi, c = divmod(step, 2)
                 nxt = pi + 1
+                far = pi + TREE_LEAD
+                e_i = step - EB_STEP
                 if c == 0:
-                    if pi + 2 < N_PAIRS:
-                        load_k(pi + 2)
                     if nxt < N_PAIRS:
-                        load_q(nxt)
                         load_v(nxt)
-                if c == 1 and pi >= 1:
-                    eb_sub(pi - 1)
+                    if far + 1 < N_PAIRS:
+                        load_k(far + 1)
+                    if nxt + 1 < N_PAIRS:
+                        load_q(nxt + 1)
+                    if pi in (0, 1):
+                        load_bias(pi)
+                    if far - 1 < N_PAIRS:
+                        turn_mk(far - 1)
+                if 0 <= e_i < 8:
+                    eb_sub(e_i)
                 if step + 1 < N_UNITS:
                     sub(step + 1)
                 exps(step)
-                if c == 0:
+                if step + 1 < B:
                     eq(step + 1)
-                    if 2 <= nxt < N_PAIRS:
-                        tree1(nxt)
+                if 0 <= e_i < 8:
+                    eb_exp(e_i)
+                if c == 0:
+                    if far - 1 < N_PAIRS:
+                        reduce_mk(far - 1)
                     if step >= 1:
                         cast_ek(step - 1)
-                    if 2 <= nxt < N_PAIRS:
-                        tree2(nxt)
+                    if far < N_PAIRS:
+                        tree1(far)
                     if step >= 1:
                         mul_v(step - 1)
-                    if 2 <= nxt < N_PAIRS:
-                        tree3(nxt)
+                    if far < N_PAIRS:
+                        tree2(far)
                     if step >= 2:
                         qz(step - 2)
-                    if pi in (1, 2):
-                        bias_max(pi - 1, 2)
-                    if 2 <= nxt < N_PAIRS:
-                        reduce_mk(nxt)
-                    if pi in (1, 2):
-                        bias_max(pi - 1, 3)
+                    if far < N_PAIRS:
+                        tree3(far)
+                    if pi in (2, 3):
+                        bias_max(pi - 2, 2)
+                        bias_max(pi - 2, 3)
                 else:
-                    if step + 1 < B:
-                        eq(step + 1)
-                    if pi >= 1:
-                        eb_exp(pi - 1)
-                    if pi in (0, 1):
-                        bias_max(pi, 0)
+                    if pi in (1, 2):
+                        bias_max(pi - 1, 0)
                     cast_ek(step - 1)
-                    if pi in (0, 1):
-                        bias_max(pi, 1)
+                    if pi in (1, 2):
+                        bias_max(pi - 1, 1)
                     mul_v(step - 1)
-                    if nxt < N_PAIRS and on_vector(nxt, 1):
-                        sub_on_vector(nxt)
                     if step >= 2:
                         qz(step - 2)
-                    if pi >= 2:
-                        eb_qz(pi - 2)
-                if step == MX0_STEP:
-                    mx(0)
-            tstep(0)
-            eb_sub(7)
-            eb_exp(7)
-            mx(1)
-            ars(0)
-            mx(2)
+                if 0 <= e_i - 2 < 8:
+                    eb_qz(e_i - 2)
             cast_ek(N_UNITS - 1)
-            mul_v(N_UNITS - 1)
             eb_qz(6)
+            mul_v(N_UNITS - 1)
             qz(N_UNITS - 2)
-            qz(N_UNITS - 1)
             eb_qz(7)
+            qz(N_UNITS - 1)
 
-        with tc.tile_pool(name="ost", bufs=3) as opool:
+        with tc.tile_pool(name="ost", bufs=4) as opool:
+            order = [("R", i) for i in range(R_FIRST)]
+            for i in range(R_FIRST, 16):
+                order.extend([("R", i), ("P", i - R_FIRST)])
+            order.extend([("P", i) for i in range(16 - R_FIRST, 16)])
+            n_tiles = len(order)
 
-            def fin(s):
-                quad, m = divmod(s, 8)
+            def store(tile):
+                quad, m = place(tile)
                 out_v = out[4 * quad : 4 * quad + 4].rearrange("b (p m) d -> p b m d", m=8)
-                if m % 4 == 0:
-                    osts[s // 4] = opool.tile([P, 4, 4, D], F32, name="ost", tag="ost")
-                ost = osts[s // 4]
-                nc.vector.tensor_tensor(
-                    out=ost[:, :, m % 4, :],
-                    in0=nums[s][:].rearrange("p (b d) -> p b d", b=4),
-                    in1=tts[s][:],
-                    op=ALU.mult,
-                )
-                if s >= N_STEPS2 - 8:
+                ost = osts[(quad, m // 4)]
+                if tile[0] == "P" and tile[1] >= 16 - SINGLE:
                     nc.sync.dma_start(out=out_v[:, :, m : m + 1, :], in_=ost[:, :, m % 4 : m % 4 + 1, :])
-                elif m % 4 == 3:
-                    nc.sync.dma_start(out=out_v[:, :, m - 3 : m + 1, :], in_=ost[:])
+                elif m % 2 == 1:
+                    nc.sync.dma_start(out=out_v[:, :, m - 1 : m + 1, :], in_=ost[:, :, m % 4 - 1 : m % 4 + 1, :])
 
-            for s in range(1, N_STEPS2 + 3):
-                if 3 <= s < N_STEPS2:
-                    mx(s)
-                if s < N_STEPS2:
-                    tstep(s)
-                    ars(s)
-                if s - 1 < N_STEPS2:
-                    square(s - 1)
-                if s >= 3:
-                    fin(s - 3)
+            def last(tile):
+                quad, m = place(tile)
+                key = (quad, m // 4)
+                if key not in osts:
+                    osts[key] = opool.tile([P, 4, 4, D], F32, name="ost", tag="ost")
+                ost = osts[key]
+                if tile[0] == "R":
+                    if two_muls(tile):
+                        nc.gpsimd.tensor_tensor(out=gate(tile), in0=gate(tile), in1=ats[tile][:], op=ALU.mult)
+                    nc.gpsimd.tensor_tensor(out=ost[:, :, m % 4, :], in0=gate(tile), in1=ats[tile][:], op=ALU.mult)
+                else:
+                    mx(tile, "num")
+                    nc.vector.tensor_tensor(
+                        out=ost[:, :, m % 4, :],
+                        in0=banks[(tile, "num")][:].rearrange("p (b d) -> p b d", b=4),
+                        in1=gate(tile),
+                        op=ALU.mult,
+                    )
+                store(tile)
+
+            vq = []
+            for i in range(16):
+                vq.append(("first", ("P", i)))
+                for j in (2 * i, 2 * i + 1):
+                    if j < 16:
+                        vq.append(("first", ("R", j)))
+                if i >= FIN_LAG:
+                    vq.append(("last", ("P", i - FIN_LAG)))
+            for i in range(16 - FIN_LAG, 16):
+                vq.append(("last", ("P", i)))
+            emitted = set()
+            waiting_g = []
+
+            def emit_v():
+                what, tile = vq[0]
+                if what == "last" and ("square", tile) not in emitted:
+                    return False
+                vq.remove(vq[0])
+                if what == "first":
+                    mx(tile, "num" if tile[0] == "R" else "den")
+                    first(tile)
+                else:
+                    last(tile)
+                emitted.add((what, tile))
+                return True
+
+            def emit_g():
+                for tile in list(waiting_g):
+                    if ("first", tile) in emitted and ("square", tile) in emitted:
+                        last(tile)
+                        waiting_g.remove(tile)
+
+            for n in range(n_tiles + 1):
+                if n < n_tiles:
+                    tile = order[n]
+                    if tile[0] == "R":
+                        mx(tile, "den")
+                        waiting_g.append(tile)
+                    while tile[0] == "P" and ("first", tile) not in emitted:
+                        emit_v()
+                    ars(tile)
+                if n >= 1:
+                    square(order[n - 1])
+                    emitted.add(("square", order[n - 1]))
+                if n >= R_FIRST - 2:
+                    for i in range(2):
+                        if len(vq) > 0:
+                            emit_v()
+                emit_g()
+            while len(vq) > 0:
+                emit_v()
+            emit_g()

@@ -26,6 +26,7 @@ R_FIRST = 8
 TWO_MULS = ()
 EB_STEP = 8
 FIN_LAG = 3
+G_SQUARES = (10, 12, 14)
 SINGLE = 4
 
 
@@ -142,7 +143,9 @@ def tile_modelnew_kernel(tc, q, k, v, bias, out):
             return tile[0] == "R" and tile[1] % 4 in TWO_MULS
 
         def square(tile):
-            if tile[0] == "P":
+            if tile[0] == "P" and tile[1] in G_SQUARES:
+                nc.gpsimd.tensor_tensor(out=gate(tile), in0=gate(tile), in1=gate(tile), op=ALU.mult)
+            elif tile[0] == "P":
                 nc.scalar.activation(out=gate(tile), in_=gate(tile), func=ACT.Square)
             elif not two_muls(tile):
                 nc.scalar.activation(out=ats[tile][:], in_=ats[tile][:], func=ACT.Square)

@@ -22,10 +22,11 @@ N_PAIRS = B // 2
 N_UNITS = 2 * N_PAIRS
 HALF = N // 2
 TREE_LEAD = 3
-R_FIRST = 8
+R_FIRST = 10
 TWO_MULS = ()
 EB_STEP = 8
 FIN_LAG = 3
+D_ON_SCALAR = (7, 13)
 G_SQUARES = (10, 12, 14)
 SINGLE = 4
 
@@ -72,6 +73,7 @@ def tile_modelnew_kernel(tc, q, k, v, bias, out):
         xbs = {}
         ekfs = {}
         grps = {}
+        gds = {}
         ebts = {}
         ebgs = {}
         banks = {}
@@ -234,11 +236,21 @@ def tile_modelnew_kernel(tc, q, k, v, bias, out):
                     nc.scalar.activation(
                         out=ef[:, bi, :, :], in_=xbs[(u, bi)][:].rearrange("p (t d) -> p d t", t=4), func=ACT.Exp
                     )
+                if u in D_ON_SCALAR:
+                    gd = wk.tile([P, 2, 512], BF16, name="gd", tag="gd", bufs=1, align_bytes=64)
+                    gds[u] = gd
+                    for bi in range(2):
+                        nc.scalar.activation(
+                            out=gd[:, bi, :].rearrange("p (d t) -> p d t", t=4),
+                            in_=xbs[(u, bi)][:].rearrange("p (t d) -> p d t", t=4),
+                            func=ACT.Exp,
+                        )
 
             def cast_ek(u):
                 g = wk.tile([P, 2, 2, 512], BF16, name="grp", tag="grp", bufs=3, align_bytes=64)
                 grps[u] = g
-                nc.vector.tensor_copy(out=g[:, 1, :, :], in_=ekfs[u][:].rearrange("p b d t -> p b (d t)"))
+                if u not in D_ON_SCALAR:
+                    nc.vector.tensor_copy(out=g[:, 1, :, :], in_=ekfs[u][:].rearrange("p b d t -> p b (d t)"))
 
             def mul_v(u):
                 pi, c = divmod(u, 2)
@@ -257,7 +269,11 @@ def tile_modelnew_kernel(tc, q, k, v, bias, out):
                     nc.vector.quantize_mx(
                         out=x_codes[:, quad, c, kind, 256 * h : 256 * h + 256].bitcast(FP8X4),
                         scales=x_scales[:, quad, c, kind, 256 * h : 256 * h + 256],
-                        in_=g[:, kind, :, :].rearrange("p b x -> p (b x)"),
+                        in_=(
+                            gds[u][:].rearrange("p b x -> p (b x)")
+                            if kind == 1 and u in D_ON_SCALAR
+                            else g[:, kind, :, :].rearrange("p b x -> p (b x)")
+                        ),
                     )
 
             def eq(b):

@@ -504,7 +504,7 @@ def tile_modelnew_kernel(tc, q, k, v, bias, out):
                 if n >= 1:
                     square(order[n - 1])
                     emitted.add(("square", order[n - 1]))
-                if n >= R_FIRST - 2:
+                if n >= R_FIRST:
                     for i in range(2):
                         if len(vq) > 0:
                             emit_v()

@@ -29,6 +29,7 @@ FIN_LAG = 3
 D_ON_SCALAR = (7, 13)
 G_SQUARES = (10, 12, 14)
 SINGLE = 4
+RUN = 4
 
 
 def tile_modelnew_kernel(tc, q, k, v, bias, out):
@@ -230,12 +231,10 @@ def tile_modelnew_kernel(tc, q, k, v, bias, out):
                     nc.tensor.matmul(xb[:], lhsT=ident[:], rhs=kts[pi][:, bi, c, :], start=False, stop=True)
 
             def exps(u):
-                ef = wk.tile([P, 2, D, 4], F32, name="ekf", tag="ekf", bufs=5)
+                ef = wk.tile([P, 2, 512], F32, name="ekf", tag="ekf", bufs=5)
                 ekfs[u] = ef
                 for bi in range(2):
-                    nc.scalar.activation(
-                        out=ef[:, bi, :, :], in_=xbs[(u, bi)][:].rearrange("p (t d) -> p d t", t=4), func=ACT.Exp
-                    )
+                    nc.scalar.activation(out=ef[:, bi, :], in_=xbs[(u, bi)][:], func=ACT.Exp)
                 if u in D_ON_SCALAR:
                     gd = wk.tile([P, 2, 512], BF16, name="gd", tag="gd", bufs=1, align_bytes=64)
                     gds[u] = gd
@@ -250,16 +249,20 @@ def tile_modelnew_kernel(tc, q, k, v, bias, out):
                 g = wk.tile([P, 2, 2, 512], BF16, name="grp", tag="grp", bufs=3, align_bytes=64)
                 grps[u] = g
                 if u not in D_ON_SCALAR:
-                    nc.vector.tensor_copy(out=g[:, 1, :, :], in_=ekfs[u][:].rearrange("p b d t -> p b (d t)"))
+                    nc.vector.tensor_copy(
+                        out=g[:, 1, :, :].rearrange("p b (c i t) -> p b c t i", i=RUN, t=4),
+                        in_=ekfs[u][:].rearrange("p b (t c i) -> p b c t i", t=4, i=RUN),
+                    )
 
             def mul_v(u):
                 pi, c = divmod(u, 2)
-                nc.vector.tensor_tensor(
-                    out=grps[u][:, 0, :, :].rearrange("p b (d t) -> p b d t", t=4),
-                    in0=ekfs[u][:],
-                    in1=vts[pi][:, :, c, :].rearrange("p b (t d) -> p b d t", t=4),
-                    op=ALU.mult,
-                )
+                for bi in range(2):
+                    nc.vector.tensor_tensor(
+                        out=grps[u][:, 0, bi, :].rearrange("p (c i t) -> p c t i", i=RUN, t=4),
+                        in0=ekfs[u][:, bi, :].rearrange("p (t c i) -> p c t i", t=4, i=RUN),
+                        in1=vts[pi][:, bi, c, :].rearrange("p (t c i) -> p c t i", t=4, i=RUN),
+                        op=ALU.mult,
+                    )
 
             def qz(u):
                 pi, c = divmod(u, 2)

@@ -26,7 +26,7 @@ R_FIRST = 10
 TWO_MULS = ()
 EB_STEP = 8
 FIN_LAG = 3
-D_ON_SCALAR = (7, 13)
+D_ON_SCALAR = ()
 G_SQUARES = (10, 12, 14)
 SINGLE = 4
 RUN = 4

@@ -372,16 +372,19 @@ def tile_modelnew_kernel(tc, q, k, v, bias, out):
                 far = pi + TREE_LEAD
                 e_i = step - EB_STEP
                 if c == 0:
+                    if nxt + 1 < N_PAIRS and pi != 2:
+                        load_q(nxt + 1)
                     if nxt < N_PAIRS:
                         load_v(nxt)
                     if far + 1 < N_PAIRS:
                         load_k(far + 1)
-                    if nxt + 1 < N_PAIRS:
-                        load_q(nxt + 1)
-                    if pi in (0, 1):
-                        load_bias(pi)
+                    if pi == 0:
+                        load_bias(0)
                     if far - 1 < N_PAIRS:
                         turn_mk(far - 1)
+                if step == 3:
+                    load_q(4)
+                    load_bias(1)
                 if 0 <= e_i < 8:
                     eb_sub(e_i)
                 if step + 1 < N_UNITS:

from contextlib import ExitStack

import concourse.mybir as mybir
from concourse.masks import make_identity

F32 = mybir.dt.float32
BF16 = mybir.dt.bfloat16
U32 = mybir.dt.uint32
U8 = mybir.dt.uint8
FP8X4 = mybir.dt.float8_e4m3fn_x4
ACT = mybir.ActivationFunctionType
ALU = mybir.AluOpType
AX = mybir.AxisListType

P = 128
B = 16
N = 1024
D = 128
FLOPS = 2 * 2 * B * N * N * D

N_PAIRS = B // 2
N_UNITS = 2 * N_PAIRS
HALF = N // 2
TREE_LEAD = 3
R_FIRST = 10
TWO_MULS = ()
EB_STEP = 8
FIN_LAG = 3
D_ON_SCALAR = ()
G_SQUARES = (10, 12, 14)
SINGLE = 4
RUN = 4


def tile_modelnew_kernel(tc, q, k, v, bias, out):
    nc = tc.nc
    with ExitStack() as ctx:
        keep = ctx.enter_context(tc.tile_pool(name="keep", bufs=1))
        tpool = ctx.enter_context(tc.tile_pool(name="tpool", bufs=8))
        kpool = ctx.enter_context(tc.tile_pool(name="kpool", bufs=5))
        psx = ctx.enter_context(tc.psum_pool(name="psx", bufs=4))
        pst = ctx.enter_context(tc.psum_pool(name="pst", bufs=2))
        psm = ctx.enter_context(tc.psum_pool(name="psm", bufs=1))
        ctx.enter_context(
            tc.manual_schedule(
                engines={
                    mybir.EngineType.DVE,
                    mybir.EngineType.Activation,
                    mybir.EngineType.SP,
                    mybir.EngineType.Pool,
                }
            )
        )

        ident = keep.tile([P, P], BF16, name="ident", tag="ident")
        ident_f = keep.tile([P, P], F32, name="ident_f", tag="ident_f")
        negmb = keep.tile([P, 8], F32, name="negmb", tag="negmb")
        eb_codes = keep.tile([P, 8, 256], U32, name="eb_codes", tag="eb_codes", align_bytes=64)
        eb_scales = keep.tile([P, 8, 256], U8, name="eb_scales", tag="eb_scales", align_bytes=64)
        x_codes = keep.tile([P, 4, 2, 2, 512], U32, name="x_codes", tag="x_codes", align_bytes=64)
        x_scales = keep.tile([P, 4, 2, 2, 512], U8, name="x_scales", tag="x_scales", align_bytes=64)
        e_all = keep.tile([P, B, N], F32, name="e_all", tag="e_all")

        make_identity(nc, ident[:])
        make_identity(nc, ident_f[:])

        kts = {}
        vts = {}
        qts = {}
        mkt = {}
        trees = {}
        bms = {}
        negmk = {}
        xbs = {}
        ekfs = {}
        grps = {}
        gds = {}
        ebts = {}
        ebgs = {}
        banks = {}
        ats = {}
        osts = {}
        done = {}
        counts = {"den": 0, "num": 0}

        def place(tile):
            kind, i = tile
            quad, r = divmod(i, 4)
            return quad, (r if kind == "R" else 4 + r)

        def gate(tile):
            quad, m = place(tile)
            return e_all[:, 4 * quad : 4 * quad + 4, D * m : D * m + D]

        def mx(tile, which):
            quad, m = place(tile)
            if tile[0] == "R" and which == "den":
                bank = pst.tile([P, 512], F32, name="for_scalar", tag="tr")
            else:
                cnt = counts["den"]
                counts["den"] = cnt + 1
                if cnt % 6 == 4:
                    bank = psm.tile([P, 512], F32, name="for_vector", tag="mxa")
                elif cnt % 6 == 5:
                    bank = psm.tile([P, 512], F32, name="for_vector", tag="mxb")
                else:
                    bank = psx.tile([P, 512], F32, name="for_vector", tag="x")
            banks[(tile, which)] = bank
            kind = 1 if which == "den" else 0
            for c in range(2):
                nc.tensor.matmul_mx(
                    out=bank[:],
                    lhsT=eb_codes[:, m, 128 * c : 128 * c + 128].bitcast(FP8X4),
                    lhsT_scale=eb_scales[:, m, 128 * c : 128 * c + 128],
                    rhs=x_codes[:, quad, c, kind, :].bitcast(FP8X4),
                    rhs_scale=x_scales[:, quad, c, kind, :],
                    start=(c == 0),
                    stop=(c == 1),
                )

        def first(tile):
            bank = banks[(tile, "num" if tile[0] == "R" else "den")]
            nc.vector.scalar_tensor_tensor(
                out=gate(tile),
                in0=gate(tile),
                scalar=1.0,
                in1=bank[:].rearrange("p (b d) -> p b d", b=4),
                op0=ALU.add,
                op1=ALU.mult,
            )

        def ars(tile):
            if tile[0] == "R":
                at = kpool.tile([P, 4, D], F32, name="at", tag="at", bufs=10, offset=0)
                ats[tile] = at
                nc.scalar.activation(
                    out=at[:],
                    in_=banks[(tile, "den")][:].rearrange("p (b d) -> p b d", b=4),
                    func=ACT.Abs_reciprocal_sqrt,
                    scale=2.0,
                )
            else:
                nc.scalar.activation(out=gate(tile), in_=gate(tile), func=ACT.Abs_reciprocal_sqrt)

        def two_muls(tile):
            return tile[0] == "R" and tile[1] % 4 in TWO_MULS

        def square(tile):
            if tile[0] == "P" and tile[1] in G_SQUARES:
                nc.gpsimd.tensor_tensor(out=gate(tile), in0=gate(tile), in1=gate(tile), op=ALU.mult)
            elif tile[0] == "P":
                nc.scalar.activation(out=gate(tile), in_=gate(tile), func=ACT.Square)
            elif not two_muls(tile):
                nc.scalar.activation(out=ats[tile][:], in_=ats[tile][:], func=ACT.Square)

        with ExitStack() as ph1:
            ld = ph1.enter_context(tc.tile_pool(name="ld", bufs=3))
            wk = ph1.enter_context(tc.tile_pool(name="wk", bufs=2))

            bias_sb = wk.tile([P, 8, N], BF16, name="bias_sb", tag="bias_sb", bufs=1)
            bias_v = bias.rearrange("(p m) j -> p m j", m=8)

            def load_k(pi):
                kt = kpool.tile([P, 2, 2, 512], BF16, name="kt", tag="kt", bufs=5, offset=0)
                kts[pi] = kt
                nc.sync.dma_start(
                    out=kt[:],
                    in_=k[2 * pi : 2 * pi + 2].rearrange("b (c p t) d -> p b c (t d)", c=2, p=P, t=4),
                )

            def load_v(pi):
                vt = ld.tile([P, 2, 2, 512], BF16, name="vt", tag="vt")
                vts[pi] = vt
                nc.sync.dma_start(
                    out=vt[:],
                    in_=v[2 * pi : 2 * pi + 2].rearrange("b (c p t) d -> p b c (t d)", c=2, p=P, t=4),
                )

            def load_q(pi):
                qt = ld.tile([P, 2, N], BF16, name="qt", tag="qt", bufs=3)
                qts[pi] = qt
                nc.sync.dma_start(
                    out=qt[:], in_=q[2 * pi : 2 * pi + 2].rearrange("b (p m) d -> p b (m d)", m=8)
                )

            def load_bias(h):
                nc.sync.dma_start(out=bias_sb[:, 4 * h : 4 * h + 4, :], in_=bias_v[:, 4 * h : 4 * h + 4, :])

            def tree1(pi):
                m1 = wk.tile([P, 2, 512], BF16, name="m1", tag="m1")
                trees[(pi, 1)] = m1
                nc.vector.tensor_tensor(out=m1[:], in0=kts[pi][:, :, 0, :], in1=kts[pi][:, :, 1, :], op=ALU.max)

            def tree2(pi):
                m1 = trees[(pi, 1)]
                m2 = wk.tile([P, 2, 256], BF16, name="m2", tag="m2")
                trees[(pi, 2)] = m2
                nc.vector.tensor_tensor(out=m2[:], in0=m1[:, :, 0:256], in1=m1[:, :, 256:512], op=ALU.max)

            def tree3(pi):
                m2 = trees[(pi, 2)]
                m3 = wk.tile([P, 2, 128], BF16, name="m3", tag="m3", bufs=3)
                trees[(pi, 3)] = m3
                nc.vector.tensor_tensor(out=m3[:], in0=m2[:, :, 0:128], in1=m2[:, :, 128:256], op=ALU.max)

            def turn_mk(pi):
                tb = pst.tile([P, 2, P], BF16, name="mkt", tag="tr")
                mkt[pi] = tb
                for bi in range(2):
                    nc.tensor.transpose(tb[:, bi, :], trees[(pi, 3)][:, bi, :], ident[:])

            def reduce_mk(pi):
                nm = wk.tile([P, 2], F32, name="negmk", tag="negmk", bufs=5)
                negmk[pi] = nm
                nc.vector.tensor_reduce(out=nm[:], in_=mkt[pi][:], axis=AX.X, op=ALU.max, negate=True)

            def sub(u):
                pi, c = divmod(u, 2)
                for bi in range(2):
                    xb = psx.tile([P, 512], F32, name="xb", tag="x")
                    xbs[(u, bi)] = xb
                    for t in range(4):
                        nc.tensor.matmul(
                            xb[:, D * t : D * t + D],
                            lhsT=negmk[pi][:, bi : bi + 1].to_broadcast([P, P]),
                            rhs=ident_f[:],
                            is_transpose=True,
                            start=(t == 0),
                            stop=False,
                        )
                    nc.tensor.matmul(xb[:], lhsT=ident[:], rhs=kts[pi][:, bi, c, :], start=False, stop=True)

            def exps(u):
                ef = wk.tile([P, 2, 512], F32, name="ekf", tag="ekf", bufs=5)
                ekfs[u] = ef
                for bi in range(2):
                    nc.scalar.activation(out=ef[:, bi, :], in_=xbs[(u, bi)][:], func=ACT.Exp)
                if u in D_ON_SCALAR:
                    gd = wk.tile([P, 2, 512], BF16, name="gd", tag="gd", bufs=1, align_bytes=64)
                    gds[u] = gd
                    for bi in range(2):
                        nc.scalar.activation(
                            out=gd[:, bi, :].rearrange("p (d t) -> p d t", t=4),
                            in_=xbs[(u, bi)][:].rearrange("p (t d) -> p d t", t=4),
                            func=ACT.Exp,
                        )

            def cast_ek(u):
                g = wk.tile([P, 2, 2, 512], BF16, name="grp", tag="grp", bufs=3, align_bytes=64)
                grps[u] = g
                if u not in D_ON_SCALAR:
                    nc.vector.tensor_copy(
                        out=g[:, 1, :, :].rearrange("p b (c i t) -> p b c t i", i=RUN, t=4),
                        in_=ekfs[u][:].rearrange("p b (t c i) -> p b c t i", t=4, i=RUN),
                    )

            def mul_v(u):
                pi, c = divmod(u, 2)
                for bi in range(2):
                    nc.vector.tensor_tensor(
                        out=grps[u][:, 0, bi, :].rearrange("p (c i t) -> p c t i", i=RUN, t=4),
                        in0=ekfs[u][:, bi, :].rearrange("p (t c i) -> p c t i", t=4, i=RUN),
                        in1=vts[pi][:, bi, c, :].rearrange("p (t c i) -> p c t i", t=4, i=RUN),
                        op=ALU.mult,
                    )

            def qz(u):
                pi, c = divmod(u, 2)
                quad, h = divmod(pi, 2)
                g = grps[u]
                for kind in range(2):
                    nc.vector.quantize_mx(
                        out=x_codes[:, quad, c, kind, 256 * h : 256 * h + 256].bitcast(FP8X4),
                        scales=x_scales[:, quad, c, kind, 256 * h : 256 * h + 256],
                        in_=(
                            gds[u][:].rearrange("p b x -> p (b x)")
                            if kind == 1 and u in D_ON_SCALAR
                            else g[:, kind, :, :].rearrange("p b x -> p (b x)")
                        ),
                    )

            def eq(b):
                nc.scalar.activation(
                    out=e_all[:, b, 0:HALF], in_=qts[b // 2][:, b % 2, 0:HALF], func=ACT.Tanh, scale=0.5
                )
                nc.scalar.activation(
                    out=e_all[:, b, HALF:N], in_=qts[b // 2][:, b % 2, HALF:N], func=ACT.Exp, scale=-1.0
                )

            def bias_max(h, level):
                sl = slice(4 * h, 4 * h + 4)
                if level == 0:
                    b1 = wk.tile([P, 4, 512], BF16, name="b1", tag="b1", bufs=1)
                    bms[1] = b1
                    nc.vector.tensor_tensor(
                        out=b1[:], in0=bias_sb[:, sl, 0:512], in1=bias_sb[:, sl, 512:1024], op=ALU.max
                    )
                elif level == 1:
                    b2 = wk.tile([P, 4, 256], BF16, name="b2", tag="b2", bufs=1)
                    bms[2] = b2
                    nc.vector.tensor_tensor(out=b2[:], in0=bms[1][:, :, 0:256], in1=bms[1][:, :, 256:512], op=ALU.max)
                elif level == 2:
                    b3 = wk.tile([P, 4, 128], BF16, name="b3", tag="b3", bufs=1)
                    bms[3] = b3
                    nc.vector.tensor_tensor(out=b3[:], in0=bms[2][:, :, 0:128], in1=bms[2][:, :, 128:256], op=ALU.max)
                else:
                    nc.vector.tensor_reduce(out=negmb[:, sl], in_=bms[3][:], axis=AX.X, op=ALU.max, negate=True)

            def eb_sub(m):
                for c in range(2):
                    ebt = psm.tile([P, 4, P], F32, name="ebt", tag="mxa" if c == 0 else "mxb")
                    ebts[(m, c)] = ebt
                    for t in range(4):
                        nc.tensor.matmul(
                            ebt[:, t, :],
                            lhsT=negmb[:, m : m + 1].to_broadcast([P, P]),
                            rhs=ident_f[:],
                            is_transpose=True,
                            start=(t == 0),
                            stop=False,
                        )
                    for t in range(4):
                        nc.tensor.matmul(
                            ebt[:, t, :],
                            lhsT=bias_sb[:, m, 512 * c + t : 512 * c + 512 : 4],
                            rhs=ident[:],
                            start=False,
                            stop=(t == 3),
                        )

            def eb_exp(m):
                ebg = tpool.tile([P, 2, P, 4], BF16, name="ebg", tag="at", align_bytes=64)
                ebgs[m] = ebg
                for c in range(2):
                    nc.scalar.activation(
                        out=ebg[:, c, :, :], in_=ebts[(m, c)][:].rearrange("p t i -> p i t"), func=ACT.Exp
                    )

            def eb_qz(m):
                nc.vector.quantize_mx(
                    out=eb_codes[:, m, :].bitcast(FP8X4),
                    scales=eb_scales[:, m, :],
                    in_=ebgs[m][:].rearrange("p c i t -> p (c i t)"),
                )

            load_k(0)
            load_q(0)
            load_k(1)
            load_v(0)
            load_k(2)
            load_q(1)
            load_k(3)
            tree1(0)
            tree2(0)
            tree3(0)
            turn_mk(0)
            eq(0)
            reduce_mk(0)
            sub(0)
            tree1(1)
            tree2(1)
            tree3(1)
            turn_mk(1)
            reduce_mk(1)
            tree1(2)
            tree2(2)
            tree3(2)

            for step in range(N_UNITS):
                pi, c = divmod(step, 2)
                nxt = pi + 1
                far = pi + TREE_LEAD
                e_i = step - EB_STEP
                if c == 0:
                    if nxt + 1 < N_PAIRS and pi != 2:
                        load_q(nxt + 1)
                    if nxt < N_PAIRS:
                        load_v(nxt)
                    if far + 1 < N_PAIRS:
                        load_k(far + 1)
                    if pi == 0:
                        load_bias(0)
                    if far - 1 < N_PAIRS:
                        turn_mk(far - 1)
                if step == 3:
                    load_q(4)
                    load_bias(1)
                if 0 <= e_i < 8:
                    eb_sub(e_i)
                if step + 1 < N_UNITS:
                    sub(step + 1)
                exps(step)
                if step + 1 < B:
                    eq(step + 1)
                if 0 <= e_i < 8:
                    eb_exp(e_i)
                if c == 0:
                    if far - 1 < N_PAIRS:
                        reduce_mk(far - 1)
                    if step >= 1:
                        cast_ek(step - 1)
                    if far < N_PAIRS:
                        tree1(far)
                    if step >= 1:
                        mul_v(step - 1)
                    if far < N_PAIRS:
                        tree2(far)
                    if step >= 2:
                        qz(step - 2)
                    if far < N_PAIRS:
                        tree3(far)
                    if pi in (2, 3):
                        bias_max(pi - 2, 2)
                        bias_max(pi - 2, 3)
                else:
                    if pi in (1, 2):
                        bias_max(pi - 1, 0)
                    cast_ek(step - 1)
                    if pi in (1, 2):
                        bias_max(pi - 1, 1)
                    mul_v(step - 1)
                    if step >= 2:
                        qz(step - 2)
                if 0 <= e_i - 2 < 8:
                    eb_qz(e_i - 2)
            cast_ek(N_UNITS - 1)
            eb_qz(6)
            mul_v(N_UNITS - 1)
            qz(N_UNITS - 2)
            eb_qz(7)
            qz(N_UNITS - 1)

        with tc.tile_pool(name="ost", bufs=4) as opool:
            order = [("R", i) for i in range(R_FIRST)]
            for i in range(R_FIRST, 16):
                order.extend([("R", i), ("P", i - R_FIRST)])
            order.extend([("P", i) for i in range(16 - R_FIRST, 16)])
            n_tiles = len(order)

            def store(tile):
                quad, m = place(tile)
                out_v = out[4 * quad : 4 * quad + 4].rearrange("b (p m) d -> p b m d", m=8)
                ost = osts[(quad, m // 4)]
                if tile[0] == "P" and tile[1] >= 16 - SINGLE:
                    nc.sync.dma_start(out=out_v[:, :, m : m + 1, :], in_=ost[:, :, m % 4 : m % 4 + 1, :])
                elif m % 2 == 1:
                    nc.sync.dma_start(out=out_v[:, :, m - 1 : m + 1, :], in_=ost[:, :, m % 4 - 1 : m % 4 + 1, :])

            def last(tile):
                quad, m = place(tile)
                key = (quad, m // 4)
                if key not in osts:
                    osts[key] = opool.tile([P, 4, 4, D], F32, name="ost", tag="ost")
                ost = osts[key]
                if tile[0] == "R":
                    if two_muls(tile):
                        nc.gpsimd.tensor_tensor(out=gate(tile), in0=gate(tile), in1=ats[tile][:], op=ALU.mult)
                    nc.gpsimd.tensor_tensor(out=ost[:, :, m % 4, :], in0=gate(tile), in1=ats[tile][:], op=ALU.mult)
                else:
                    mx(tile, "num")
                    nc.vector.tensor_tensor(
                        out=ost[:, :, m % 4, :],
                        in0=banks[(tile, "num")][:].rearrange("p (b d) -> p b d", b=4),
                        in1=gate(tile),
                        op=ALU.mult,
                    )
                store(tile)

            vq = []
            for i in range(16):
                vq.append(("first", ("P", i)))
                for j in (2 * i, 2 * i + 1):
                    if j < 16:
                        vq.append(("first", ("R", j)))
                if i >= FIN_LAG:
                    vq.append(("last", ("P", i - FIN_LAG)))
            for i in range(16 - FIN_LAG, 16):
                vq.append(("last", ("P", i)))
            emitted = set()
            waiting_g = []

            def emit_v():
                what, tile = vq[0]
                if what == "last" and ("square", tile) not in emitted:
                    return False
                vq.remove(vq[0])
                if what == "first":
                    mx(tile, "num" if tile[0] == "R" else "den")
                    first(tile)
                else:
                    last(tile)
                emitted.add((what, tile))
                return True

            def emit_g():
                for tile in list(waiting_g):
                    if ("first", tile) in emitted and ("square", tile) in emitted:
                        last(tile)
                        waiting_g.remove(tile)

            for n in range(n_tiles + 1):
                if n < n_tiles:
                    tile = order[n]
                    if tile[0] == "R":
                        mx(tile, "den")
                        waiting_g.append(tile)
                    while tile[0] == "P" and ("first", tile) not in emitted:
                        emit_v()
                    ars(tile)
                if n >= 1:
                    square(order[n - 1])
                    emitted.add(("square", order[n - 1]))
                if n >= R_FIRST:
                    for i in range(2):
                        if len(vq) > 0:
                            emit_v()
                emit_g()
            while len(vq) > 0:
                emit_v()
            emit_g()
